import numpy as np
import ml_dtypes


def mxq(x, axis, fmt="e4m3"):
    dtype, down = {"e4m3": (ml_dtypes.float8_e4m3fn, 7), "e5m2": (ml_dtypes.float8_e5m2, 14)}[fmt]
    v = np.moveaxis(np.asarray(x, np.float32).astype(ml_dtypes.bfloat16).astype(np.float64), axis, -1)
    blocks = v.reshape(v.shape[:-1] + (-1, 32))
    amax = np.abs(blocks).max(-1, keepdims=True)
    byte = np.maximum(np.where(amax > 0, np.frexp(amax)[1] - 1 + 127, 0) - down, 1)
    scale = np.exp2(byte - 127.0)
    codes = (blocks / scale).astype(np.float32).astype(dtype).astype(np.float64)
    return np.moveaxis((codes * scale).reshape(v.shape), -1, axis)


WIDE = False


def mx_kscale(k):
    if not WIDE:
        return np.ones(k)
    levels = np.array([10, -10, 5, -5, 0])
    a = np.random.permutation(np.resize(levels, k // 512 * 4)).reshape(k // 512, 4)
    idx = np.arange(k)
    return np.exp2(a[idx // 512, idx % 128 // 32])


BF16 = ml_dtypes.bfloat16


def bf(x):
    return np.asarray(x, np.float32).astype(BF16)


def f64(x):
    return np.asarray(x).astype(np.float64)


E2M1 = np.array([0.0, 0.5, 1.0, 1.5, 2.0, 3.0, 4.0, 6.0, -0.0, -0.5, -1.0, -1.5, -2.0, -3.0, -4.0, -6.0])


def pack_weight(w, fmt):
    k, n = w.shape
    w = f64(bf(w)).reshape(k // 32, 32, n)
    amax = np.abs(w).max(1)
    if fmt == "e4m3":
        byte = np.frexp(amax)[1] - 1 + 127 - 7
    else:
        mant, ex = np.frexp(amax / 6.0)
        byte = np.where(mant > 0.5, ex, ex - 1) + 127
    byte = np.clip(np.where(amax > 0, byte, 1), 1, 254)
    scaled = (w * np.exp2(127.0 - byte)[:, None, :]).reshape(k, n).astype(np.float32)
    by_word = np.ascontiguousarray(scaled.reshape(k // 512, 128, 4, n).transpose(0, 1, 3, 2))
    if fmt == "e4m3":
        words = by_word.astype(ml_dtypes.float8_e4m3fn).view(np.uint8)
    else:
        c = by_word.astype(ml_dtypes.float4_e2m1fn).view(np.uint8) & 0xF
        words = c[..., 0::2] | (c[..., 1::2] << 4)
    return np.ascontiguousarray(words), np.ascontiguousarray(byte.astype(np.uint8).reshape(k // 512, 16, n))


def unpack_weight(words, scales, fmt):
    g, p, n, _ = words.shape
    if fmt == "e4m3":
        vals = np.ascontiguousarray(words).view(ml_dtypes.float8_e4m3fn).astype(np.float64)
    else:
        nib = np.empty((g, p, n, 4), np.uint8)
        nib[..., 0::2] = words & 0xF
        nib[..., 1::2] = words >> 4
        vals = E2M1[nib]
    vals = vals * np.repeat(np.exp2(scales.astype(np.float64) - 127.0), 8, axis=1)[..., None]
    return vals.transpose(0, 1, 3, 2).reshape(g * 512, n)

def pack4(w):
    words, scales = pack_weight(w, "e2m1")
    return words.reshape(words.shape[0], 128, -1), scales


def unpack4(words, scales):
    return unpack_weight(words.reshape(words.shape[0], 128, -1, 2), scales, "e2m1")


B, S, D, H, DH, F = 1, 128, 8192, 8, 128, 4096
INNER = H * DH
HALF = DH // 2
EPS = 1e-5


def rmsnorm(u, g):
    var = np.mean(np.square(u), axis=-1, keepdims=True)
    return u * (1.0 / np.sqrt(var + EPS)) * g


def rope_interleaved(u, cos, sin):
    u1 = u[..., 0::2]
    u2 = u[..., 1::2]
    c = cos[None, :, None, :]
    s = sin[None, :, None, :]
    o1 = u1 * c - u2 * s
    o2 = u2 * c + u1 * s
    return np.stack([o1, o2], axis=-1).reshape(u.shape)


def setup_inputs():
    s = mx_kscale(D)
    ang = np.random.uniform(0.0, 2.0 * np.pi, (S, HALF))
    hidden_states = bf(np.random.standard_normal((B, S, D)) * s)
    w_q_words, w_q_scales = pack4(np.random.standard_normal((D, INNER)) * 0.02 / np.sqrt(D) / s[:, None])
    w_k_words, w_k_scales = pack4(np.random.standard_normal((D, INNER)) * 0.02 / np.sqrt(D) / s[:, None])
    w_v_words, w_v_scales = pack4(np.random.standard_normal((D, INNER)) * 3.0 / np.sqrt(D) / s[:, None])
    return {"hidden_states": hidden_states,
            "w_q_words": w_q_words,
            "w_q_scales": w_q_scales,
            "w_k_words": w_k_words,
            "w_k_scales": w_k_scales,
            "w_v_words": w_v_words,
            "w_v_scales": w_v_scales,
            "norm_q_w": bf(1.0 + 0.1 * np.random.standard_normal(DH)),
            "norm_k_w": bf(1.0 + 0.1 * np.random.standard_normal(DH)),
            "cos": bf(np.cos(ang)),
            "sin": bf(np.sin(ang))}


def reference(hidden_states, w_q_words, w_q_scales, w_k_words, w_k_scales, w_v_words, w_v_scales, norm_q_w, norm_k_w, cos, sin):
    xq = mxq(f64(hidden_states), 2, "e4m3")
    q = (xq @ unpack4(w_q_words, w_q_scales)).reshape(B, S, H, DH)
    k = (xq @ unpack4(w_k_words, w_k_scales)).reshape(B, S, H, DH)
    v = (xq @ unpack4(w_v_words, w_v_scales)).reshape(B, S, H, DH)
    q = rmsnorm(q, f64(norm_q_w))
    k = rmsnorm(k, f64(norm_k_w))
    q = rope_interleaved(q, f64(cos), f64(sin))
    k = rope_interleaved(k, f64(cos), f64(sin))
    return q, k, v

@@ -1,0 +1,223 @@
+from contextlib import ExitStack
+
+import concourse.masks as masks
+import concourse.mybir as mybir
+
+F32 = mybir.dt.float32
+BF16 = mybir.dt.bfloat16
+I32 = mybir.dt.int32
+U32 = mybir.dt.uint32
+U8 = mybir.dt.uint8
+FP8X4 = mybir.dt.float8_e4m3fn_x4
+FP4X4 = mybir.dt.float4_e2m1fn_x4
+ALU = mybir.AluOpType
+ACT = mybir.ActivationFunctionType
+
+P = 128
+D_MODEL = 8192
+HEADS = 8
+HEAD_DIM = 128
+PAIRS = HEAD_DIM // 2
+INNER = HEADS * HEAD_DIM
+EPS = 1e-5
+
+K_PASS = 4 * P
+PASSES = D_MODEL // K_PASS
+N_PASS = 512
+HALVES = INNER // N_PASS
+HEADS_PER_HALF = HEADS // HALVES
+
+X_CHUNK_PASSES = 4
+X_CHUNKS = PASSES // X_CHUNK_PASSES
+WORD_PASSES_PER_DMA = 2
+SCALE_PASSES_PER_DMA = 8
+
+FLOPS = 2 * P * D_MODEL * 3 * INNER
+
+
+def load_weight(nc, plane_pool, words_pool, w_words, w_scales):
+    plane = plane_pool.tile([P, PASSES, INNER], U8, align_bytes=64)
+    nc.vector.memset(plane[:].bitcast(I32), 0)
+    rows = w_scales.rearrange("g (far q) n -> far q g n", far=2)
+    for first in range(0, PASSES, SCALE_PASSES_PER_DMA):
+        some = slice(first, first + SCALE_PASSES_PER_DMA)
+        for q in range(8):
+            partition = 32 * (q // 4) + q % 4
+            nc.sync.dma_start(
+                out=plane[partition:P:64, some, :].bitcast(I32),
+                in_=rows[:, q, some, :].bitcast(I32),
+            )
+    words = []
+    for first in range(0, PASSES, WORD_PASSES_PER_DMA):
+        chunk = words_pool.tile([P, WORD_PASSES_PER_DMA, 2 * INNER], U8, align_bytes=64)
+        nc.sync.dma_start(
+            out=chunk[:].bitcast(I32),
+            in_=w_words[first : first + WORD_PASSES_PER_DMA].rearrange("g p b -> p g b").bitcast(I32),
+        )
+        words.append(chunk)
+    return plane, words
+
+
+def quantise_x_chunk(nc, xt_pool, grouped_pool, identity, x_chunk, codes, scales):
+    x_words = x_chunk[:].bitcast(F32)
+    grouped = grouped_pool.tile([P, X_CHUNK_PASSES * K_PASS], BF16, align_bytes=64)
+    grouped_words = grouped[:].bitcast(F32).rearrange("p (g r u) -> p g r u", g=X_CHUNK_PASSES, u=2)
+    for bank in range(X_CHUNK_PASSES // 2):
+        xt = xt_pool.tile([P, 2, 2, P], F32)
+        for j in range(2):
+            g = 2 * bank + j
+            for u in range(2):
+                nc.tensor.transpose(xt[:, j, u, :], x_words[:, 256 * g + u : 256 * (g + 1) : 2], identity[:])
+        side_by_side = xt[:].rearrange("p g u r -> p g r u")
+        if bank == 0:
+            nc.vector.tensor_copy(out=grouped_words[:, 2 * bank : 2 * bank + 2], in_=side_by_side)
+        else:
+            nc.scalar.copy(out=grouped_words[:, 2 * bank : 2 * bank + 2], in_=side_by_side)
+    nc.vector.quantize_mx(out=codes.bitcast(FP8X4), scales=scales, in_=grouped[:])
+
+
+def project(nc, acc_pool, x_codes, x_scales, plane, words):
+    acc = [acc_pool.tile([P, N_PASS], F32, name="acc%d" % half, tag="acc%d" % half) for half in range(HALVES)]
+    for c, chunk in enumerate(words):
+        for half in range(HALVES):
+            for j in range(WORD_PASSES_PER_DMA):
+                g = c * WORD_PASSES_PER_DMA + j
+                tokens = slice(g * P, (g + 1) * P)
+                nc.tensor.matmul_mx(
+                    out=acc[half][:],
+                    lhsT=x_codes[:, tokens].bitcast(FP8X4),
+                    lhsT_scale=x_scales[:, tokens],
+                    rhs=chunk[:, j, 2 * N_PASS * half : 2 * N_PASS * (half + 1)].bitcast(FP4X4),
+                    rhs_scale=plane[:, g, N_PASS * half : N_PASS * (half + 1)],
+                    start=(g == 0),
+                    stop=(g == PASSES - 1),
+                )
+    return acc
+
+
+def norm_and_rotate(nc, work, acc, gain_cos, gain_sin, out_rows):
+    squares = work.tile([P, INNER], F32)
+    for half in range(HALVES):
+        nc.scalar.activation(out=squares[:, N_PASS * half : N_PASS * (half + 1)], in_=acc[half][:], func=ACT.Square)
+    with_cos = work.tile([P, 2, HEADS, PAIRS], F32)
+    with_sin = work.tile([P, 2, HEADS, PAIRS], F32)
+    over_heads = [P, 2, HEADS_PER_HALF, PAIRS]
+    for half in range(HALVES):
+        heads = slice(HEADS_PER_HALF * half, HEADS_PER_HALF * (half + 1))
+        by_parity = acc[half][:].rearrange("p (h i e) -> p e h i", h=HEADS_PER_HALF, e=2)
+        nc.vector.tensor_tensor(
+            out=with_cos[:, :, heads, :], in0=by_parity, in1=gain_cos[:].unsqueeze(2).to_broadcast(over_heads), op=ALU.mult
+        )
+        nc.vector.tensor_tensor(
+            out=with_sin[:, :, heads, :], in0=by_parity, in1=gain_sin[:].unsqueeze(2).to_broadcast(over_heads), op=ALU.mult
+        )
+    sum_sq = work.tile([P, HEADS], F32)
+    nc.vector.tensor_reduce(
+        out=sum_sq[:], in_=squares[:].rearrange("p (h d) -> p h d", h=HEADS), axis=mybir.AxisListType.X, op=ALU.add
+    )
+    mean_sq = work.tile([P, HEADS], F32)
+    nc.vector.tensor_scalar(out=mean_sq[:], in0=sum_sq[:], scalar1=1.0 / HEAD_DIM, scalar2=EPS, op0=ALU.mult, op1=ALU.add)
+    rms = work.tile([P, HEADS], F32)
+    nc.scalar.sqrt(rms[:], mean_sq[:])
+    rotated = work.tile([P, 2, HEADS, PAIRS], F32)
+    nc.vector.tensor_sub(out=rotated[:, 0], in0=with_cos[:, 0], in1=with_sin[:, 1])
+    nc.vector.tensor_add(out=rotated[:, 1], in0=with_cos[:, 1], in1=with_sin[:, 0])
+    inv_rms = work.tile([P, HEADS], F32)
+    nc.vector.reciprocal(inv_rms[:], rms[:])
+    result = work.tile([P, HEADS, PAIRS, 2], F32)
+    nc.vector.tensor_tensor(
+        out=result[:],
+        in0=rotated[:].rearrange("p e h i -> p h i e"),
+        in1=inv_rms[:].unsqueeze(2).unsqueeze(3).to_broadcast([P, HEADS, PAIRS, 2]),
+        op=ALU.mult,
+    )
+    nc.scalar.dma_start(out=out_rows, in_=result[:].rearrange("p h i e -> p (h i e)"))
+
+
+def tile_flux2parallelselfattention_pa_k_kernel(
+    tc,
+    hidden_states,
+    w_q_words,
+    w_q_scales,
+    w_k_words,
+    w_k_scales,
+    w_v_words,
+    w_v_scales,
+    norm_q_w,
+    norm_k_w,
+    cos,
+    sin,
+    out_0,
+    out_1,
+    out_2,
+):
+    nc = tc.nc
+    with ExitStack() as ctx:
+        keep = ctx.enter_context(tc.tile_pool(name="keep", bufs=1))
+        x_pool = ctx.enter_context(tc.tile_pool(name="x", bufs=X_CHUNKS))
+        grouped_pool = ctx.enter_context(tc.tile_pool(name="grouped", bufs=2))
+        plane_pool = ctx.enter_context(tc.tile_pool(name="planes", bufs=3))
+        words_pool = ctx.enter_context(tc.tile_pool(name="words", bufs=3 * PASSES // WORD_PASSES_PER_DMA))
+        work = ctx.enter_context(tc.tile_pool(name="work", bufs=1))
+        acc_pool = ctx.enter_context(tc.psum_pool(name="acc", bufs=2))
+        xt_pool = ctx.enter_context(tc.psum_pool(name="xt", bufs=3))
+        gains_pool = ctx.enter_context(tc.psum_pool(name="gains", bufs=1))
+        ctx.enter_context(tc.manual_schedule())
+
+        identity = keep.tile([P, P], F32)
+        masks.make_identity(nc, identity[:])
+        ones = keep.tile([P, P], BF16)
+        nc.gpsimd.memset(ones[:], 1.0)
+        gains_row = keep.tile([P, 2 * HEAD_DIM], BF16)
+        nc.gpsimd.memset(gains_row[:], 0.0)
+        cos_sb = keep.tile([P, PAIRS], BF16)
+        nc.scalar.dma_start(out=cos_sb[:], in_=cos)
+        sin_sb = keep.tile([P, PAIRS], BF16)
+        nc.scalar.dma_start(out=sin_sb[:], in_=sin)
+        nc.scalar.dma_start(out=gains_row[0:1, 0:HEAD_DIM], in_=norm_q_w.rearrange("(o d) -> o d", o=1))
+        nc.scalar.dma_start(out=gains_row[0:1, HEAD_DIM : 2 * HEAD_DIM], in_=norm_k_w.rearrange("(o d) -> o d", o=1))
+
+        x_rows = hidden_states.rearrange("b s d -> (b s) d")
+        x_chunks = []
+        for c in range(X_CHUNKS):
+            x_chunk = x_pool.tile([P, X_CHUNK_PASSES * K_PASS], BF16)
+            nc.sync.dma_start(out=x_chunk[:], in_=x_rows[:, c * X_CHUNK_PASSES * K_PASS : (c + 1) * X_CHUNK_PASSES * K_PASS])
+            x_chunks.append(x_chunk)
+        q_plane, q_words = load_weight(nc, plane_pool, words_pool, w_q_words, w_q_scales)
+
+        x_codes = keep.tile([P, PASSES * P], U32, align_bytes=64)
+        x_scales = keep.tile([P, PASSES * P], U8, align_bytes=64)
+        for c in range(X_CHUNKS):
+            columns = slice(c * X_CHUNK_PASSES * P, (c + 1) * X_CHUNK_PASSES * P)
+            quantise_x_chunk(nc, xt_pool, grouped_pool, identity, x_chunks[c], x_codes[:, columns], x_scales[:, columns])
+
+        k_plane, k_words = load_weight(nc, plane_pool, words_pool, w_k_words, w_k_scales)
+        v_plane, v_words = load_weight(nc, plane_pool, words_pool, w_v_words, w_v_scales)
+
+        gains = gains_pool.tile([P, 2 * HEAD_DIM], F32)
+        nc.tensor.matmul(out=gains[:], lhsT=ones[:], rhs=gains_row[:], start=True, stop=True)
+        tables = []
+        for w in range(2):
+            by_parity = gains[:, w * HEAD_DIM : (w + 1) * HEAD_DIM].rearrange("p (i e) -> p e i", e=2)
+            gain_cos = keep.tile([P, 2, PAIRS], F32, name="gain_cos%d" % w)
+            nc.vector.tensor_tensor(
+                out=gain_cos[:], in0=by_parity, in1=cos_sb[:].unsqueeze(1).to_broadcast([P, 2, PAIRS]), op=ALU.mult
+            )
+            gain_sin = keep.tile([P, 2, PAIRS], F32, name="gain_sin%d" % w)
+            nc.vector.tensor_tensor(
+                out=gain_sin[:], in0=by_parity, in1=sin_sb[:].unsqueeze(1).to_broadcast([P, 2, PAIRS]), op=ALU.mult
+            )
+            tables.append((gain_cos, gain_sin))
+
+        q_acc = project(nc, acc_pool, x_codes, x_scales, q_plane, q_words)
+        norm_and_rotate(nc, work, q_acc, tables[0][0], tables[0][1], out_0.rearrange("b s h d -> (b s) (h d)"))
+        k_acc = project(nc, acc_pool, x_codes, x_scales, k_plane, k_words)
+        norm_and_rotate(nc, work, k_acc, tables[1][0], tables[1][1], out_1.rearrange("b s h d -> (b s) (h d)"))
+
+        v_acc = project(nc, acc_pool, x_codes, x_scales, v_plane, v_words)
+        v_rows = out_2.rearrange("b s h d -> (b s) (h d)")
+        values = work.tile([P, INNER], F32)
+        nc.scalar.copy(out=values[:, 0:N_PASS], in_=v_acc[0][:])
+        nc.scalar.dma_start(out=v_rows[:, 0:N_PASS], in_=values[:, 0:N_PASS])
+        nc.vector.tensor_copy(out=values[:, N_PASS:INNER], in_=v_acc[1][:])
+        nc.sync.dma_start(out=v_rows[:, N_PASS:INNER], in_=values[:, N_PASS:INNER])

@@ -30,23 +30,21 @@ HEADS_PER_HALF = HEADS // HALVES
 X_CHUNK_PASSES = 4
 X_CHUNKS = PASSES // X_CHUNK_PASSES
 WORD_PASSES_PER_DMA = 2
-SCALE_PASSES_PER_DMA = 8
 
 FLOPS = 2 * P * D_MODEL * 3 * INNER
 
 
-def load_weight(nc, plane_pool, words_pool, w_words, w_scales):
+def load_scales(nc, plane_pool, w_scales):
     plane = plane_pool.tile([P, PASSES, INNER], U8, align_bytes=64)
     nc.vector.memset(plane[:].bitcast(I32), 0)
     rows = w_scales.rearrange("g (far q) n -> far q g n", far=2)
-    for first in range(0, PASSES, SCALE_PASSES_PER_DMA):
-        some = slice(first, first + SCALE_PASSES_PER_DMA)
-        for q in range(8):
-            partition = 32 * (q // 4) + q % 4
-            nc.sync.dma_start(
-                out=plane[partition:P:64, some, :].bitcast(I32),
-                in_=rows[:, q, some, :].bitcast(I32),
-            )
+    for q in range(8):
+        partition = 32 * (q // 4) + q % 4
+        nc.sync.dma_start(out=plane[partition:P:64, :, :].bitcast(I32), in_=rows[:, q, :, :].bitcast(I32))
+    return plane
+
+
+def load_words(nc, words_pool, w_words):
     words = []
     for first in range(0, PASSES, WORD_PASSES_PER_DMA):
         chunk = words_pool.tile([P, WORD_PASSES_PER_DMA, 2 * INNER], U8, align_bytes=64)
@@ -55,7 +53,7 @@ def load_weight(nc, plane_pool, words_pool, w_words, w_scales):
             in_=w_words[first : first + WORD_PASSES_PER_DMA].rearrange("g p b -> p g b").bitcast(I32),
         )
         words.append(chunk)
-    return plane, words
+    return words
 
 
 def quantise_x_chunk(nc, xt_pool, grouped_pool, identity, x_chunk, codes, scales):
@@ -183,16 +181,18 @@ def tile_flux2parallelselfattention_pa_k_kernel(
             x_chunk = x_pool.tile([P, X_CHUNK_PASSES * K_PASS], BF16)
             nc.sync.dma_start(out=x_chunk[:], in_=x_rows[:, c * X_CHUNK_PASSES * K_PASS : (c + 1) * X_CHUNK_PASSES * K_PASS])
             x_chunks.append(x_chunk)
-        q_plane, q_words = load_weight(nc, plane_pool, words_pool, w_q_words, w_q_scales)
+        q_plane = load_scales(nc, plane_pool, w_q_scales)
+        k_plane = load_scales(nc, plane_pool, w_k_scales)
+        v_plane = load_scales(nc, plane_pool, w_v_scales)
+        q_words = load_words(nc, words_pool, w_q_words)
+        k_words = load_words(nc, words_pool, w_k_words)
+        v_words = load_words(nc, words_pool, w_v_words)
 
         x_codes = keep.tile([P, PASSES * P], U32, align_bytes=64)
         x_scales = keep.tile([P, PASSES * P], U8, align_bytes=64)
         for c in range(X_CHUNKS):
             columns = slice(c * X_CHUNK_PASSES * P, (c + 1) * X_CHUNK_PASSES * P)
             quantise_x_chunk(nc, xt_pool, grouped_pool, identity, x_chunks[c], x_codes[:, columns], x_scales[:, columns])
-
-        k_plane, k_words = load_weight(nc, plane_pool, words_pool, w_k_words, w_k_scales)
-        v_plane, v_words = load_weight(nc, plane_pool, words_pool, w_v_words, w_v_scales)
 
         gains = gains_pool.tile([P, 2 * HEAD_DIM], F32)
         nc.tensor.matmul(out=gains[:], lhsT=ones[:], rhs=gains_row[:], start=True, stop=True)

@@ -37,10 +37,9 @@ FLOPS = 2 * P * D_MODEL * 3 * INNER
 def load_scales(nc, plane_pool, w_scales):
     plane = plane_pool.tile([P, PASSES, INNER], U8, align_bytes=64)
     nc.vector.memset(plane[:].bitcast(I32), 0)
-    rows = w_scales.rearrange("g (far q) n -> far q g n", far=2)
-    for q in range(8):
-        partition = 32 * (q // 4) + q % 4
-        nc.sync.dma_start(out=plane[partition:P:64, :, :].bitcast(I32), in_=rows[:, q, :, :].bitcast(I32))
+    rows = w_scales.rearrange("g (quadrant r) n -> quadrant r g n", r=4)
+    for r in range(4):
+        nc.sync.dma_start(out=plane[r:P:32, :, :].bitcast(I32), in_=rows[:, r, :, :].bitcast(I32))
     return plane
 
 

@@ -37,9 +37,10 @@ FLOPS = 2 * P * D_MODEL * 3 * INNER
 def load_scales(nc, plane_pool, w_scales):
     plane = plane_pool.tile([P, PASSES, INNER], U8, align_bytes=64)
     nc.vector.memset(plane[:].bitcast(I32), 0)
-    rows = w_scales.rearrange("g (quadrant r) n -> quadrant r g n", r=4)
-    for r in range(4):
-        nc.sync.dma_start(out=plane[r:P:32, :, :].bitcast(I32), in_=rows[:, r, :, :].bitcast(I32))
+    rows = w_scales.rearrange("g (far q) n -> far q g n", far=2)
+    for q in range(8):
+        partition = 32 * (q // 4) + q % 4
+        nc.sync.dma_start(out=plane[partition:P:64, :, :].bitcast(I32), in_=rows[:, q, :, :].bitcast(I32))
     return plane
 
 
@@ -92,7 +93,7 @@ def project(nc, acc_pool, x_codes, x_scales, plane, words):
     return acc
 
 
-def norm_and_rotate(nc, work, acc, gain_cos, gain_sin, out_rows):
+def norm_and_rotate(nc, work, result_pool, acc, gain_cos, gain_sin, out_rows):
     squares = work.tile([P, INNER], F32)
     for half in range(HALVES):
         nc.scalar.activation(out=squares[:, N_PASS * half : N_PASS * (half + 1)], in_=acc[half][:], func=ACT.Square)
@@ -121,14 +122,14 @@ def norm_and_rotate(nc, work, acc, gain_cos, gain_sin, out_rows):
     nc.vector.tensor_add(out=rotated[:, 1], in0=with_cos[:, 1], in1=with_sin[:, 0])
     inv_rms = work.tile([P, HEADS], F32)
     nc.vector.reciprocal(inv_rms[:], rms[:])
-    result = work.tile([P, HEADS, PAIRS, 2], F32)
+    result = result_pool.tile([P, HEADS, PAIRS, 2], F32)
     nc.vector.tensor_tensor(
         out=result[:],
         in0=rotated[:].rearrange("p e h i -> p h i e"),
         in1=inv_rms[:].unsqueeze(2).unsqueeze(3).to_broadcast([P, HEADS, PAIRS, 2]),
         op=ALU.mult,
     )
-    nc.scalar.dma_start(out=out_rows, in_=result[:].rearrange("p h i e -> p (h i e)"))
+    nc.sync.dma_start(out=out_rows, in_=result[:].rearrange("p h i e -> p (h i e)"))
 
 
 def tile_flux2parallelselfattention_pa_k_kernel(
@@ -156,6 +157,7 @@ def tile_flux2parallelselfattention_pa_k_kernel(
         plane_pool = ctx.enter_context(tc.tile_pool(name="planes", bufs=3))
         words_pool = ctx.enter_context(tc.tile_pool(name="words", bufs=3 * PASSES // WORD_PASSES_PER_DMA))
         work = ctx.enter_context(tc.tile_pool(name="work", bufs=1))
+        result_pool = ctx.enter_context(tc.tile_pool(name="results", bufs=2))
         acc_pool = ctx.enter_context(tc.psum_pool(name="acc", bufs=2))
         xt_pool = ctx.enter_context(tc.psum_pool(name="xt", bufs=3))
         gains_pool = ctx.enter_context(tc.psum_pool(name="gains", bufs=1))
@@ -209,9 +211,9 @@ def tile_flux2parallelselfattention_pa_k_kernel(
             tables.append((gain_cos, gain_sin))
 
         q_acc = project(nc, acc_pool, x_codes, x_scales, q_plane, q_words)
-        norm_and_rotate(nc, work, q_acc, tables[0][0], tables[0][1], out_0.rearrange("b s h d -> (b s) (h d)"))
+        norm_and_rotate(nc, work, result_pool, q_acc, tables[0][0], tables[0][1], out_0.rearrange("b s h d -> (b s) (h d)"))
         k_acc = project(nc, acc_pool, x_codes, x_scales, k_plane, k_words)
-        norm_and_rotate(nc, work, k_acc, tables[1][0], tables[1][1], out_1.rearrange("b s h d -> (b s) (h d)"))
+        norm_and_rotate(nc, work, result_pool, k_acc, tables[1][0], tables[1][1], out_1.rearrange("b s h d -> (b s) (h d)"))
 
         v_acc = project(nc, acc_pool, x_codes, x_scales, v_plane, v_words)
         v_rows = out_2.rearrange("b s h d -> (b s) (h d)")

@@ -37,10 +37,14 @@ FLOPS = 2 * P * D_MODEL * 3 * INNER
 def load_scales(nc, plane_pool, w_scales):
     plane = plane_pool.tile([P, PASSES, INNER], U8, align_bytes=64)
     nc.vector.memset(plane[:].bitcast(I32), 0)
-    rows = w_scales.rearrange("g (far q) n -> far q g n", far=2)
-    for q in range(8):
-        partition = 32 * (q // 4) + q % 4
-        nc.sync.dma_start(out=plane[partition:P:64, :, :].bitcast(I32), in_=rows[:, q, :, :].bitcast(I32))
+    rows = w_scales.rearrange("g (o q) n -> o q g n", o=1)
+    for q in range(16):
+        row = 8 * (q % 2) + q // 2
+        partition = 32 * (row // 4) + row % 4
+        nc.sync.dma_start(
+            out=plane[partition : partition + 1, :, :].bitcast(I32),
+            in_=rows[:, row, :, :].bitcast(I32),
+        )
     return plane
 
 

@@ -34,29 +34,34 @@ WORD_PASSES_PER_DMA = 2
 FLOPS = 2 * P * D_MODEL * 3 * INNER
 
 
-def load_scales(nc, plane_pool, w_scales):
+def make_plane(engine, plane_pool):
     plane = plane_pool.tile([P, PASSES, INNER], U8, align_bytes=64)
-    nc.vector.memset(plane[:].bitcast(I32), 0)
-    rows = w_scales.rearrange("g (o q) n -> o q g n", o=1)
-    for q in range(16):
-        row = 8 * (q % 2) + q // 2
-        partition = 32 * (row // 4) + row % 4
-        nc.sync.dma_start(
-            out=plane[partition : partition + 1, :, :].bitcast(I32),
-            in_=rows[:, row, :, :].bitcast(I32),
-        )
+    engine.memset(plane[:].bitcast(I32), 0)
     return plane
 
 
-def load_words(nc, words_pool, w_words):
+def load_scale_row(nc, plane, w_scales, row):
+    partition = 32 * (row // 4) + row % 4
+    rows = w_scales.rearrange("g (o q) n -> o q g n", o=1)
+    nc.sync.dma_start(out=plane[partition : partition + 1, :, :].bitcast(I32), in_=rows[:, row, :, :].bitcast(I32))
+
+
+SCALE_ROW_ORDER = [8 * (i % 2) + i // 2 for i in range(16)]
+
+
+def load_words_and_scales(nc, words_pool, w_words, plane, w_scales):
     words = []
-    for first in range(0, PASSES, WORD_PASSES_PER_DMA):
+    for c in range(PASSES // WORD_PASSES_PER_DMA):
+        first = c * WORD_PASSES_PER_DMA
         chunk = words_pool.tile([P, WORD_PASSES_PER_DMA, 2 * INNER], U8, align_bytes=64)
         nc.sync.dma_start(
             out=chunk[:].bitcast(I32),
             in_=w_words[first : first + WORD_PASSES_PER_DMA].rearrange("g p b -> p g b").bitcast(I32),
         )
         words.append(chunk)
+        if plane is not None:
+            for row in SCALE_ROW_ORDER[2 * c : 2 * c + 2]:
+                load_scale_row(nc, plane, w_scales, row)
     return words
 
 
@@ -186,12 +191,14 @@ def tile_flux2parallelselfattention_pa_k_kernel(
             x_chunk = x_pool.tile([P, X_CHUNK_PASSES * K_PASS], BF16)
             nc.sync.dma_start(out=x_chunk[:], in_=x_rows[:, c * X_CHUNK_PASSES * K_PASS : (c + 1) * X_CHUNK_PASSES * K_PASS])
             x_chunks.append(x_chunk)
-        q_plane = load_scales(nc, plane_pool, w_q_scales)
-        k_plane = load_scales(nc, plane_pool, w_k_scales)
-        v_plane = load_scales(nc, plane_pool, w_v_scales)
-        q_words = load_words(nc, words_pool, w_q_words)
-        k_words = load_words(nc, words_pool, w_k_words)
-        v_words = load_words(nc, words_pool, w_v_words)
+        q_plane = make_plane(nc.vector, plane_pool)
+        k_plane = make_plane(nc.gpsimd, plane_pool)
+        v_plane = make_plane(nc.gpsimd, plane_pool)
+        for row in SCALE_ROW_ORDER:
+            load_scale_row(nc, q_plane, w_q_scales, row)
+        q_words = load_words_and_scales(nc, words_pool, w_q_words, k_plane, w_k_scales)
+        k_words = load_words_and_scales(nc, words_pool, w_k_words, v_plane, w_v_scales)
+        v_words = load_words_and_scales(nc, words_pool, w_v_words, None, None)
 
         x_codes = keep.tile([P, PASSES * P], U32, align_bytes=64)
         x_scales = keep.tile([P, PASSES * P], U8, align_bytes=64)

from contextlib import ExitStack

import concourse.masks as masks
import concourse.mybir as mybir

F32 = mybir.dt.float32
BF16 = mybir.dt.bfloat16
I32 = mybir.dt.int32
U32 = mybir.dt.uint32
U8 = mybir.dt.uint8
FP8X4 = mybir.dt.float8_e4m3fn_x4
FP4X4 = mybir.dt.float4_e2m1fn_x4
ALU = mybir.AluOpType
ACT = mybir.ActivationFunctionType

P = 128
D_MODEL = 8192
HEADS = 8
HEAD_DIM = 128
PAIRS = HEAD_DIM // 2
INNER = HEADS * HEAD_DIM
EPS = 1e-5

K_PASS = 4 * P
PASSES = D_MODEL // K_PASS
N_PASS = 512
HALVES = INNER // N_PASS
HEADS_PER_HALF = HEADS // HALVES

X_CHUNK_PASSES = 4
X_CHUNKS = PASSES // X_CHUNK_PASSES
WORD_PASSES_PER_DMA = 2

FLOPS = 2 * P * D_MODEL * 3 * INNER


def make_plane(engine, plane_pool):
    plane = plane_pool.tile([P, PASSES, INNER], U8, align_bytes=64)
    engine.memset(plane[:].bitcast(I32), 0)
    return plane


def load_scale_row(nc, plane, w_scales, row):
    partition = 32 * (row // 4) + row % 4
    rows = w_scales.rearrange("g (o q) n -> o q g n", o=1)
    nc.sync.dma_start(out=plane[partition : partition + 1, :, :].bitcast(I32), in_=rows[:, row, :, :].bitcast(I32))


SCALE_ROW_ORDER = [8 * (i % 2) + i // 2 for i in range(16)]


def load_words_and_scales(nc, words_pool, w_words, plane, w_scales):
    words = []
    for c in range(PASSES // WORD_PASSES_PER_DMA):
        first = c * WORD_PASSES_PER_DMA
        chunk = words_pool.tile([P, WORD_PASSES_PER_DMA, 2 * INNER], U8, align_bytes=64)
        nc.sync.dma_start(
            out=chunk[:].bitcast(I32),
            in_=w_words[first : first + WORD_PASSES_PER_DMA].rearrange("g p b -> p g b").bitcast(I32),
        )
        words.append(chunk)
        if plane is not None:
            for row in SCALE_ROW_ORDER[2 * c : 2 * c + 2]:
                load_scale_row(nc, plane, w_scales, row)
    return words


def quantise_x_chunk(nc, xt_pool, grouped_pool, identity, x_chunk, codes, scales):
    x_words = x_chunk[:].bitcast(F32)
    grouped = grouped_pool.tile([P, X_CHUNK_PASSES * K_PASS], BF16, align_bytes=64)
    grouped_words = grouped[:].bitcast(F32).rearrange("p (g r u) -> p g r u", g=X_CHUNK_PASSES, u=2)
    for bank in range(X_CHUNK_PASSES // 2):
        xt = xt_pool.tile([P, 2, 2, P], F32)
        for j in range(2):
            g = 2 * bank + j
            for u in range(2):
                nc.tensor.transpose(xt[:, j, u, :], x_words[:, 256 * g + u : 256 * (g + 1) : 2], identity[:])
        side_by_side = xt[:].rearrange("p g u r -> p g r u")
        if bank == 0:
            nc.vector.tensor_copy(out=grouped_words[:, 2 * bank : 2 * bank + 2], in_=side_by_side)
        else:
            nc.scalar.copy(out=grouped_words[:, 2 * bank : 2 * bank + 2], in_=side_by_side)
    nc.vector.quantize_mx(out=codes.bitcast(FP8X4), scales=scales, in_=grouped[:])


def project(nc, acc_pool, x_codes, x_scales, plane, words):
    acc = [acc_pool.tile([P, N_PASS], F32, name="acc%d" % half, tag="acc%d" % half) for half in range(HALVES)]
    for c, chunk in enumerate(words):
        for half in range(HALVES):
            for j in range(WORD_PASSES_PER_DMA):
                g = c * WORD_PASSES_PER_DMA + j
                tokens = slice(g * P, (g + 1) * P)
                nc.tensor.matmul_mx(
                    out=acc[half][:],
                    lhsT=x_codes[:, tokens].bitcast(FP8X4),
                    lhsT_scale=x_scales[:, tokens],
                    rhs=chunk[:, j, 2 * N_PASS * half : 2 * N_PASS * (half + 1)].bitcast(FP4X4),
                    rhs_scale=plane[:, g, N_PASS * half : N_PASS * (half + 1)],
                    start=(g == 0),
                    stop=(g == PASSES - 1),
                )
    return acc


def norm_and_rotate(nc, work, result_pool, acc, gain_cos, gain_sin, out_rows):
    squares = work.tile([P, INNER], F32)
    for half in range(HALVES):
        nc.scalar.activation(out=squares[:, N_PASS * half : N_PASS * (half + 1)], in_=acc[half][:], func=ACT.Square)
    with_cos = work.tile([P, 2, HEADS, PAIRS], F32)
    with_sin = work.tile([P, 2, HEADS, PAIRS], F32)
    over_heads = [P, 2, HEADS_PER_HALF, PAIRS]
    for half in range(HALVES):
        heads = slice(HEADS_PER_HALF * half, HEADS_PER_HALF * (half + 1))
        by_parity = acc[half][:].rearrange("p (h i e) -> p e h i", h=HEADS_PER_HALF, e=2)
        nc.vector.tensor_tensor(
            out=with_cos[:, :, heads, :], in0=by_parity, in1=gain_cos[:].unsqueeze(2).to_broadcast(over_heads), op=ALU.mult
        )
        nc.vector.tensor_tensor(
            out=with_sin[:, :, heads, :], in0=by_parity, in1=gain_sin[:].unsqueeze(2).to_broadcast(over_heads), op=ALU.mult
        )
    sum_sq = work.tile([P, HEADS], F32)
    nc.vector.tensor_reduce(
        out=sum_sq[:], in_=squares[:].rearrange("p (h d) -> p h d", h=HEADS), axis=mybir.AxisListType.X, op=ALU.add
    )
    mean_sq = work.tile([P, HEADS], F32)
    nc.vector.tensor_scalar(out=mean_sq[:], in0=sum_sq[:], scalar1=1.0 / HEAD_DIM, scalar2=EPS, op0=ALU.mult, op1=ALU.add)
    rms = work.tile([P, HEADS], F32)
    nc.scalar.sqrt(rms[:], mean_sq[:])
    rotated = work.tile([P, 2, HEADS, PAIRS], F32)
    nc.vector.tensor_sub(out=rotated[:, 0], in0=with_cos[:, 0], in1=with_sin[:, 1])
    nc.vector.tensor_add(out=rotated[:, 1], in0=with_cos[:, 1], in1=with_sin[:, 0])
    inv_rms = work.tile([P, HEADS], F32)
    nc.vector.reciprocal(inv_rms[:], rms[:])
    result = result_pool.tile([P, HEADS, PAIRS, 2], F32)
    nc.vector.tensor_tensor(
        out=result[:],
        in0=rotated[:].rearrange("p e h i -> p h i e"),
        in1=inv_rms[:].unsqueeze(2).unsqueeze(3).to_broadcast([P, HEADS, PAIRS, 2]),
        op=ALU.mult,
    )
    nc.sync.dma_start(out=out_rows, in_=result[:].rearrange("p h i e -> p (h i e)"))


def tile_flux2parallelselfattention_pa_k_kernel(
    tc,
    hidden_states,
    w_q_words,
    w_q_scales,
    w_k_words,
    w_k_scales,
    w_v_words,
    w_v_scales,
    norm_q_w,
    norm_k_w,
    cos,
    sin,
    out_0,
    out_1,
    out_2,
):
    nc = tc.nc
    with ExitStack() as ctx:
        keep = ctx.enter_context(tc.tile_pool(name="keep", bufs=1))
        x_pool = ctx.enter_context(tc.tile_pool(name="x", bufs=X_CHUNKS))
        grouped_pool = ctx.enter_context(tc.tile_pool(name="grouped", bufs=2))
        plane_pool = ctx.enter_context(tc.tile_pool(name="planes", bufs=3))
        words_pool = ctx.enter_context(tc.tile_pool(name="words", bufs=3 * PASSES // WORD_PASSES_PER_DMA))
        work = ctx.enter_context(tc.tile_pool(name="work", bufs=1))
        result_pool = ctx.enter_context(tc.tile_pool(name="results", bufs=2))
        acc_pool = ctx.enter_context(tc.psum_pool(name="acc", bufs=2))
        xt_pool = ctx.enter_context(tc.psum_pool(name="xt", bufs=3))
        gains_pool = ctx.enter_context(tc.psum_pool(name="gains", bufs=1))
        ctx.enter_context(tc.manual_schedule())

        identity = keep.tile([P, P], F32)
        masks.make_identity(nc, identity[:])
        ones = keep.tile([P, P], BF16)
        nc.gpsimd.memset(ones[:], 1.0)
        gains_row = keep.tile([P, 2 * HEAD_DIM], BF16)
        nc.gpsimd.memset(gains_row[:], 0.0)
        cos_sb = keep.tile([P, PAIRS], BF16)
        nc.scalar.dma_start(out=cos_sb[:], in_=cos)
        sin_sb = keep.tile([P, PAIRS], BF16)
        nc.scalar.dma_start(out=sin_sb[:], in_=sin)
        nc.scalar.dma_start(out=gains_row[0:1, 0:HEAD_DIM], in_=norm_q_w.rearrange("(o d) -> o d", o=1))
        nc.scalar.dma_start(out=gains_row[0:1, HEAD_DIM : 2 * HEAD_DIM], in_=norm_k_w.rearrange("(o d) -> o d", o=1))

        x_rows = hidden_states.rearrange("b s d -> (b s) d")
        x_chunks = []
        for c in range(X_CHUNKS):
            x_chunk = x_pool.tile([P, X_CHUNK_PASSES * K_PASS], BF16)
            nc.sync.dma_start(out=x_chunk[:], in_=x_rows[:, c * X_CHUNK_PASSES * K_PASS : (c + 1) * X_CHUNK_PASSES * K_PASS])
            x_chunks.append(x_chunk)
        q_plane = make_plane(nc.vector, plane_pool)
        k_plane = make_plane(nc.gpsimd, plane_pool)
        v_plane = make_plane(nc.gpsimd, plane_pool)
        for row in SCALE_ROW_ORDER:
            load_scale_row(nc, q_plane, w_q_scales, row)
        q_words = load_words_and_scales(nc, words_pool, w_q_words, k_plane, w_k_scales)
        k_words = load_words_and_scales(nc, words_pool, w_k_words, v_plane, w_v_scales)
        v_words = load_words_and_scales(nc, words_pool, w_v_words, None, None)

        x_codes = keep.tile([P, PASSES * P], U32, align_bytes=64)
        x_scales = keep.tile([P, PASSES * P], U8, align_bytes=64)
        for c in range(X_CHUNKS):
            columns = slice(c * X_CHUNK_PASSES * P, (c + 1) * X_CHUNK_PASSES * P)
            quantise_x_chunk(nc, xt_pool, grouped_pool, identity, x_chunks[c], x_codes[:, columns], x_scales[:, columns])

        gains = gains_pool.tile([P, 2 * HEAD_DIM], F32)
        nc.tensor.matmul(out=gains[:], lhsT=ones[:], rhs=gains_row[:], start=True, stop=True)
        tables = []
        for w in range(2):
            by_parity = gains[:, w * HEAD_DIM : (w + 1) * HEAD_DIM].rearrange("p (i e) -> p e i", e=2)
            gain_cos = keep.tile([P, 2, PAIRS], F32, name="gain_cos%d" % w)
            nc.vector.tensor_tensor(
                out=gain_cos[:], in0=by_parity, in1=cos_sb[:].unsqueeze(1).to_broadcast([P, 2, PAIRS]), op=ALU.mult
            )
            gain_sin = keep.tile([P, 2, PAIRS], F32, name="gain_sin%d" % w)
            nc.vector.tensor_tensor(
                out=gain_sin[:], in0=by_parity, in1=sin_sb[:].unsqueeze(1).to_broadcast([P, 2, PAIRS]), op=ALU.mult
            )
            tables.append((gain_cos, gain_sin))

        q_acc = project(nc, acc_pool, x_codes, x_scales, q_plane, q_words)
        norm_and_rotate(nc, work, result_pool, q_acc, tables[0][0], tables[0][1], out_0.rearrange("b s h d -> (b s) (h d)"))
        k_acc = project(nc, acc_pool, x_codes, x_scales, k_plane, k_words)
        norm_and_rotate(nc, work, result_pool, k_acc, tables[1][0], tables[1][1], out_1.rearrange("b s h d -> (b s) (h d)"))

        v_acc = project(nc, acc_pool, x_codes, x_scales, v_plane, v_words)
        v_rows = out_2.rearrange("b s h d -> (b s) (h d)")
        values = work.tile([P, INNER], F32)
        nc.scalar.copy(out=values[:, 0:N_PASS], in_=v_acc[0][:])
        nc.scalar.dma_start(out=v_rows[:, 0:N_PASS], in_=values[:, 0:N_PASS])
        nc.vector.tensor_copy(out=values[:, N_PASS:INNER], in_=v_acc[1][:])
        nc.sync.dma_start(out=v_rows[:, N_PASS:INNER], in_=values[:, N_PASS:INNER])
